import numpy as np
import ml_dtypes


def mxq(x, axis, fmt="e4m3"):
    dtype, down = {"e4m3": (ml_dtypes.float8_e4m3fn, 7), "e5m2": (ml_dtypes.float8_e5m2, 14)}[fmt]
    v = np.moveaxis(np.asarray(x, np.float32).astype(ml_dtypes.bfloat16).astype(np.float64), axis, -1)
    blocks = v.reshape(v.shape[:-1] + (-1, 32))
    amax = np.abs(blocks).max(-1, keepdims=True)
    byte = np.maximum(np.where(amax > 0, np.frexp(amax)[1] - 1 + 127, 0) - down, 1)
    scale = np.exp2(byte - 127.0)
    codes = (blocks / scale).astype(np.float32).astype(dtype).astype(np.float64)
    return np.moveaxis((codes * scale).reshape(v.shape), -1, axis)


WIDE = False


def mx_kscale(k):
    if not WIDE:
        return np.ones(k)
    levels = np.array([10, -10, 5, -5, 0])
    if k % 512:
        return np.exp2(np.random.permutation(np.resize(levels, k // 32))).repeat(32)
    a = np.empty((k // 512, 16))
    for p in range(k // 512):
        a[p, :8] = np.random.permutation(np.resize(levels, 8))
        for g in range(8):
            far = levels[np.abs(levels - a[p, g]) >= 10]
            a[p, g + 8] = far[np.random.randint(len(far))]
    return np.exp2(a.ravel()).repeat(32)


BF16 = ml_dtypes.bfloat16


def bf(x):
    return np.asarray(x, np.float32).astype(BF16)


def f64(x):
    return np.asarray(x).astype(np.float64)


S, E, HQ, HK, D, C = 1024, 1024, 16, 4, 128, 512


def rotate_half(t):
    t1, t2 = np.split(t, 2, axis=-1)
    return np.concatenate([-t2, t1], axis=-1)


def setup_inputs():
    s = mx_kscale(E)
    theta = np.random.uniform(0.0, 2.0 * np.pi, (S, D // 2))
    theta = np.concatenate([theta, theta], axis=-1)
    return {"x": bf(np.random.standard_normal((S, E)) * s),
            "w_q": bf(np.random.standard_normal((HQ * D, E)) * 1.4 / np.sqrt(E) / s[None, :]),
            "w_k": bf(np.random.standard_normal((HK * D, E)) * 1.4 / np.sqrt(E) / s[None, :]),
            "w_v": bf(np.random.standard_normal((HK * D, E)) / np.sqrt(E) / s[None, :]),
            "cos_tab": bf(np.cos(theta)), "sin_tab": bf(np.sin(theta))}


def reference(x, w_q, w_k, w_v, cos_tab, sin_tab):
    xq = mxq(f64(x), 1, "e4m3")
    q = (xq @ mxq(f64(w_q), 1, "e4m3").T).reshape(S, HQ, D)
    k = (xq @ mxq(f64(w_k), 1, "e4m3").T).reshape(S, HK, D)
    v = (xq @ mxq(f64(w_v), 1, "e4m3").T).reshape(S, HK, D)
    c = f64(cos_tab).reshape(S, 1, D)
    sn = f64(sin_tab).reshape(S, 1, D)
    q_rot = q * c + rotate_half(q) * sn
    k_rot = k * c + rotate_half(k) * sn
    return q_rot, k_rot, v

@@ -1,0 +1,194 @@
+import concourse.mybir as mybir
+from concourse.masks import make_identity
+
+F32 = mybir.dt.float32
+BF16 = mybir.dt.bfloat16
+U32 = mybir.dt.uint32
+U8 = mybir.dt.uint8
+FP8X4 = mybir.dt.float8_e4m3fn_x4
+MULT = mybir.AluOpType.mult
+ADD = mybir.AluOpType.add
+
+P = 128
+ROWS = 1024
+K = 1024
+HEAD = 128
+HALF = HEAD // 2
+K_PASS = 4 * P
+PASSES = K // K_PASS
+WORDS = K // 2
+PASS_WORDS = K_PASS // 2
+ROW_TILES = ROWS // P
+CHUNK_HEADS = 4
+CHUNK = CHUNK_HEADS * HEAD
+
+FLOPS = 2 * ROWS * K * (2048 + 512 + 512)
+
+
+def tile_groupedqueryattention_pa_kernel(
+    tc, x, w_q, w_k, w_v, cos_tab, sin_tab, out_0, out_1, out_2
+):
+    nc = tc.nc
+
+    def rows_on_partitions(out):
+        return out.rearrange("(p m) h d -> p m (h d)", m=ROW_TILES)
+
+    chunks = []
+    for c in range(w_q.shape[0] // CHUNK):
+        cols = slice(c * CHUNK, (c + 1) * CHUNK)
+        chunks.append((w_q[cols, :], rows_on_partitions(out_0)[:, :, cols], True))
+    chunks.append((w_k, rows_on_partitions(out_1), True))
+    chunks.append((w_v, rows_on_partitions(out_2), False))
+
+    with tc.tile_pool(name="keep", bufs=1) as keep, tc.tile_pool(
+        name="weights", bufs=len(chunks)
+    ) as weights, tc.tile_pool(name="quant", bufs=2) as quant, tc.tile_pool(
+        name="work", bufs=3
+    ) as work, tc.psum_pool(name="flipped", bufs=4) as flipped, tc.psum_pool(
+        name="sums", bufs=4
+    ) as sums:
+        identity = keep.tile([P, P], F32)
+        make_identity(nc, identity[:])
+
+        x_raw = keep.tile([P, ROW_TILES * K], BF16)
+        x_rows = x.rearrange("(p m) k -> p (m k)", m=ROW_TILES)
+        w_raws = []
+        for c in range(len(chunks)):
+            w_raws.append(weights.tile([P, CHUNK_HEADS * K], BF16, name="w_raw"))
+
+        def load_x(m0, m1):
+            nc.sync.dma_start(out=x_raw[:, m0 * K : m1 * K], in_=x_rows[:, m0 * K : m1 * K])
+
+        def load_w(c):
+            nc.sync.dma_start(
+                out=w_raws[c][:].rearrange("p (t k) -> p t k", t=CHUNK_HEADS),
+                in_=chunks[c][0].rearrange("(t p) k -> p t k", p=P),
+            )
+
+        cos_raw = keep.tile([P, ROW_TILES, HEAD], BF16)
+        sin_raw = keep.tile([P, ROW_TILES, HEAD], BF16)
+        load_x(0, 2)
+        load_w(0)
+        nc.scalar.dma_start(out=cos_raw[:], in_=cos_tab.rearrange("(p m) d -> p m d", m=ROW_TILES))
+        nc.scalar.dma_start(out=sin_raw[:], in_=sin_tab.rearrange("(p m) d -> p m d", m=ROW_TILES))
+        for m0 in range(2, ROW_TILES, 2):
+            load_x(m0, m0 + 2)
+        for c in range(1, len(chunks)):
+            load_w(c)
+
+        factors = keep.tile([P, ROW_TILES, 2, HEAD], F32)
+        nc.gpsimd.tensor_scalar(
+            out=factors[:, :, 0, :], in0=cos_raw[:], scalar1=1.0, scalar2=0.0, op0=MULT, op1=ADD
+        )
+        nc.gpsimd.tensor_scalar(
+            out=factors[:, :, 1, 0:HALF], in0=sin_raw[:, :, HALF:HEAD],
+            scalar1=1.0, scalar2=0.0, op0=MULT, op1=ADD,
+        )
+        nc.gpsimd.tensor_scalar(
+            out=factors[:, :, 1, HALF:HEAD], in0=sin_raw[:, :, 0:HALF],
+            scalar1=-1.0, scalar2=0.0, op0=MULT, op1=ADD,
+        )
+
+        def flip(bank_plane, words, first_word):
+            nc.tensor.transpose(bank_plane, words[:, first_word : first_word + 2 * P - 1 : 2], identity[:])
+
+        x_words = x_raw[:].bitcast(F32)
+        x_grouped = keep.tile([P, ROW_TILES * K], BF16, align_bytes=64)
+        x_codes = keep.tile([P, ROW_TILES * K // 4], U32, align_bytes=64)
+        x_scales = keep.tile([P, ROW_TILES * K // 4], U8, align_bytes=64)
+
+        def prepare_x(m):
+            bank = flipped.tile([P, PASSES, 2, P], F32, name="bank")
+            for g in range(PASSES):
+                for w in range(2):
+                    flip(bank[:, g, w, :], x_words, m * WORDS + g * PASS_WORDS + w)
+            nc.scalar.copy(
+                out=x_grouped[:].bitcast(F32)[:, m * WORDS : (m + 1) * WORDS].rearrange(
+                    "p (g r w) -> p g r w", g=PASSES, w=2
+                ),
+                in_=bank[:].rearrange("p g w r -> p g r w"),
+            )
+            nc.vector.quantize_mx(
+                out=x_codes[:, m * K // 4 : (m + 1) * K // 4].bitcast(FP8X4),
+                scales=x_scales[:, m * K // 4 : (m + 1) * K // 4],
+                in_=x_grouped[:, m * K : (m + 1) * K],
+            )
+
+        def prepare_w(c):
+            w_words = w_raws[c][:].bitcast(F32)
+            w_grouped = quant.tile([P, PASSES, 4 * CHUNK], BF16, align_bytes=64)
+            w_codes = quant.tile([P, PASSES, CHUNK], U32, align_bytes=64)
+            w_scales = quant.tile([P, PASSES, CHUNK], U8, align_bytes=64)
+            for g in range(PASSES):
+                grouped_words = w_grouped[:, g, :].bitcast(F32)
+                for t0 in range(0, CHUNK_HEADS, 2):
+                    bank = flipped.tile([P, 2, 2, P], F32, name="bank")
+                    for t in range(2):
+                        for w in range(2):
+                            flip(bank[:, t, w, :], w_words, (t0 + t) * WORDS + g * PASS_WORDS + w)
+                    nc.scalar.copy(
+                        out=grouped_words[:, t0 * 2 * P : (t0 + 2) * 2 * P].rearrange(
+                            "p (t r w) -> p t r w", t=2, w=2
+                        ),
+                        in_=bank[:].rearrange("p t w r -> p t r w"),
+                    )
+                nc.vector.quantize_mx(
+                    out=w_codes[:, g, :].bitcast(FP8X4),
+                    scales=w_scales[:, g, :],
+                    in_=w_grouped[:, g, :],
+                )
+            return w_codes, w_scales
+
+        def project(m, w_codes, w_scales):
+            acc = sums.tile([P, CHUNK], F32)
+            for g in range(PASSES):
+                x_cols = slice((m * PASSES + g) * P, (m * PASSES + g + 1) * P)
+                nc.tensor.matmul_mx(
+                    out=acc[:],
+                    lhsT=x_codes[:, x_cols].bitcast(FP8X4),
+                    lhsT_scale=x_scales[:, x_cols],
+                    rhs=w_codes[:, g, :].bitcast(FP8X4),
+                    rhs_scale=w_scales[:, g, :],
+                    start=(g == 0),
+                    stop=(g == PASSES - 1),
+                )
+            return acc
+
+        for m in range(ROW_TILES):
+            prepare_x(m)
+        ready = prepare_w(0)
+
+        for c in range(len(chunks)):
+            w_codes, w_scales = ready
+            if c + 1 < len(chunks):
+                ready = prepare_w(c + 1)
+            out_rows, rotated = chunks[c][1], chunks[c][2]
+            for m0 in range(0, ROW_TILES, 2):
+                result = work.tile([P, 2, CHUNK_HEADS, HEAD], F32)
+                if rotated:
+                    products = work.tile([P, 2, 2, CHUNK_HEADS, HEAD], F32)
+                    for i in range(2):
+                        acc = project(m0 + i, w_codes, w_scales)
+                        shape = [P, 2, CHUNK_HEADS, HEAD]
+                        nc.vector.tensor_tensor(
+                            out=products[:, i],
+                            in0=acc[:].rearrange("p (h d) -> p h d", h=CHUNK_HEADS)
+                            .unsqueeze(1).to_broadcast(shape),
+                            in1=factors[:, m0 + i].unsqueeze(2).to_broadcast(shape),
+                            op=MULT,
+                        )
+                    for mine, other in ((slice(0, HALF), slice(HALF, HEAD)), (slice(HALF, HEAD), slice(0, HALF))):
+                        nc.gpsimd.tensor_tensor(
+                            out=result[:, :, :, mine],
+                            in0=products[:, :, 0, :, mine],
+                            in1=products[:, :, 1, :, other],
+                            op=ADD,
+                        )
+                else:
+                    for i in range(2):
+                        acc = project(m0 + i, w_codes, w_scales)
+                        nc.scalar.copy(out=result[:, i].rearrange("p h d -> p (h d)"), in_=acc[:])
+                nc.sync.dma_start(
+                    out=out_rows[:, m0 : m0 + 2, :],
+                    in_=result[:].rearrange("p i h d -> p i (h d)"),
+                )

@@ -16,8 +16,8 @@ HEAD = 128
 HALF = HEAD // 2
 K_PASS = 4 * P
 PASSES = K // K_PASS
-WORDS = K // 2
-PASS_WORDS = K_PASS // 2
+PAIRS = K // 2
+PASS_PAIRS = K_PASS // 2
 ROW_TILES = ROWS // P
 CHUNK_HEADS = 4
 CHUNK = CHUNK_HEADS * HEAD
@@ -33,162 +33,200 @@ def tile_groupedqueryattention_pa_kernel(
     def rows_on_partitions(out):
         return out.rearrange("(p m) h d -> p m (h d)", m=ROW_TILES)
 
-    chunks = []
+    rotated = []
     for c in range(w_q.shape[0] // CHUNK):
         cols = slice(c * CHUNK, (c + 1) * CHUNK)
-        chunks.append((w_q[cols, :], rows_on_partitions(out_0)[:, :, cols], True))
-    chunks.append((w_k, rows_on_partitions(out_1), True))
-    chunks.append((w_v, rows_on_partitions(out_2), False))
+        rotated.append((w_q[cols, :], rows_on_partitions(out_0)[:, :, cols]))
+    rotated.append((w_k, rows_on_partitions(out_1)))
+    value = (w_v, rows_on_partitions(out_2))
 
     with tc.tile_pool(name="keep", bufs=1) as keep, tc.tile_pool(
-        name="weights", bufs=len(chunks)
+        name="weights", bufs=len(rotated) + 1
     ) as weights, tc.tile_pool(name="quant", bufs=2) as quant, tc.tile_pool(
-        name="work", bufs=3
+        name="work", bufs=4
     ) as work, tc.psum_pool(name="flipped", bufs=4) as flipped, tc.psum_pool(
         name="sums", bufs=4
-    ) as sums:
+    ) as sums, tc.manual_schedule():
         identity = keep.tile([P, P], F32)
         make_identity(nc, identity[:])
 
         x_raw = keep.tile([P, ROW_TILES * K], BF16)
         x_rows = x.rearrange("(p m) k -> p (m k)", m=ROW_TILES)
-        w_raws = []
-        for c in range(len(chunks)):
-            w_raws.append(weights.tile([P, CHUNK_HEADS * K], BF16, name="w_raw"))
 
         def load_x(m0, m1):
             nc.sync.dma_start(out=x_raw[:, m0 * K : m1 * K], in_=x_rows[:, m0 * K : m1 * K])
 
-        def load_w(c):
-            nc.sync.dma_start(
-                out=w_raws[c][:].rearrange("p (t k) -> p t k", t=CHUNK_HEADS),
-                in_=chunks[c][0].rearrange("(t p) k -> p t k", p=P),
-            )
+        def load_w(chunk, parts):
+            w_raw = weights.tile([P, CHUNK_HEADS * K], BF16, name="w_raw")
+            step = CHUNK_HEADS // parts
+            for t0 in range(0, CHUNK_HEADS, step):
+                nc.sync.dma_start(
+                    out=w_raw[:, t0 * K : (t0 + step) * K].rearrange("p (t k) -> p t k", t=step),
+                    in_=chunk[0][t0 * P : (t0 + step) * P, :].rearrange("(t p) k -> p t k", p=P),
+                )
+            return w_raw
 
         cos_raw = keep.tile([P, ROW_TILES, HEAD], BF16)
         sin_raw = keep.tile([P, ROW_TILES, HEAD], BF16)
-        load_x(0, 2)
-        load_w(0)
-        nc.scalar.dma_start(out=cos_raw[:], in_=cos_tab.rearrange("(p m) d -> p m d", m=ROW_TILES))
-        nc.scalar.dma_start(out=sin_raw[:], in_=sin_tab.rearrange("(p m) d -> p m d", m=ROW_TILES))
+        load_x(0, 1)
+        w_raws = [load_w(rotated[0], 2)]
+        nc.sync.dma_start(out=cos_raw[:], in_=cos_tab.rearrange("(p m) d -> p m d", m=ROW_TILES))
+        nc.sync.dma_start(out=sin_raw[:], in_=sin_tab.rearrange("(p m) d -> p m d", m=ROW_TILES))
+        load_x(1, 2)
         for m0 in range(2, ROW_TILES, 2):
             load_x(m0, m0 + 2)
-        for c in range(1, len(chunks)):
-            load_w(c)
+        for chunk in rotated[1:4]:
+            w_raws.append(load_w(chunk, 1))
+        v_raw = load_w(value, 1)
+        w_raws.append(load_w(rotated[4], 1))
 
         factors = keep.tile([P, ROW_TILES, 2, HEAD], F32)
-        nc.gpsimd.tensor_scalar(
-            out=factors[:, :, 0, :], in0=cos_raw[:], scalar1=1.0, scalar2=0.0, op0=MULT, op1=ADD
-        )
-        nc.gpsimd.tensor_scalar(
-            out=factors[:, :, 1, 0:HALF], in0=sin_raw[:, :, HALF:HEAD],
-            scalar1=1.0, scalar2=0.0, op0=MULT, op1=ADD,
-        )
-        nc.gpsimd.tensor_scalar(
-            out=factors[:, :, 1, HALF:HEAD], in0=sin_raw[:, :, 0:HALF],
-            scalar1=-1.0, scalar2=0.0, op0=MULT, op1=ADD,
-        )
+        for tiles in (slice(0, 2), slice(2, ROW_TILES)):
+            nc.gpsimd.tensor_scalar(
+                out=factors[:, tiles, 0, :], in0=cos_raw[:, tiles, :],
+                scalar1=1.0, scalar2=0.0, op0=MULT, op1=ADD,
+            )
+            nc.gpsimd.tensor_scalar(
+                out=factors[:, tiles, 1, 0:HALF], in0=sin_raw[:, tiles, HALF:HEAD],
+                scalar1=1.0, scalar2=0.0, op0=MULT, op1=ADD,
+            )
+            nc.gpsimd.tensor_scalar(
+                out=factors[:, tiles, 1, HALF:HEAD], in0=sin_raw[:, tiles, 0:HALF],
+                scalar1=-1.0, scalar2=0.0, op0=MULT, op1=ADD,
+            )
 
-        def flip(bank_plane, words, first_word):
-            nc.tensor.transpose(bank_plane, words[:, first_word : first_word + 2 * P - 1 : 2], identity[:])
+        def flip(raw, tile, grouped, copy):
+            bank = flipped.tile([P, PASSES, 2, P], F32, name="bank")
+            words = raw[:].bitcast(F32)
+            for g in range(PASSES):
+                for w in range(2):
+                    first = tile * PAIRS + g * PASS_PAIRS + w
+                    nc.tensor.transpose(
+                        bank[:, g, w, :], words[:, first : first + PASS_PAIRS - 1 : 2], identity[:]
+                    )
+            copy(
+                out=grouped.rearrange("p g (r w) -> p g r w", w=2),
+                in_=bank[:].rearrange("p g w r -> p g r w"),
+            )
 
-        x_words = x_raw[:].bitcast(F32)
         x_grouped = keep.tile([P, ROW_TILES * K], BF16, align_bytes=64)
         x_codes = keep.tile([P, ROW_TILES * K // 4], U32, align_bytes=64)
         x_scales = keep.tile([P, ROW_TILES * K // 4], U8, align_bytes=64)
 
-        def prepare_x(m):
-            bank = flipped.tile([P, PASSES, 2, P], F32, name="bank")
-            for g in range(PASSES):
-                for w in range(2):
-                    flip(bank[:, g, w, :], x_words, m * WORDS + g * PASS_WORDS + w)
-            nc.scalar.copy(
-                out=x_grouped[:].bitcast(F32)[:, m * WORDS : (m + 1) * WORDS].rearrange(
-                    "p (g r w) -> p g r w", g=PASSES, w=2
-                ),
-                in_=bank[:].rearrange("p g w r -> p g r w"),
-            )
+        def flip_x(m):
+            words = x_grouped[:].bitcast(F32)[:, m * PAIRS : (m + 1) * PAIRS]
+            flip(x_raw, m, words.rearrange("p (g c) -> p g c", g=PASSES), nc.scalar.copy)
+
+        def quantize_x(m0, m1):
             nc.vector.quantize_mx(
-                out=x_codes[:, m * K // 4 : (m + 1) * K // 4].bitcast(FP8X4),
-                scales=x_scales[:, m * K // 4 : (m + 1) * K // 4],
-                in_=x_grouped[:, m * K : (m + 1) * K],
+                out=x_codes[:, m0 * K // 4 : m1 * K // 4].bitcast(FP8X4),
+                scales=x_scales[:, m0 * K // 4 : m1 * K // 4],
+                in_=x_grouped[:, m0 * K : m1 * K],
             )
 
-        def prepare_w(c):
-            w_words = w_raws[c][:].bitcast(F32)
-            w_grouped = quant.tile([P, PASSES, 4 * CHUNK], BF16, align_bytes=64)
-            w_codes = quant.tile([P, PASSES, CHUNK], U32, align_bytes=64)
-            w_scales = quant.tile([P, PASSES, CHUNK], U8, align_bytes=64)
-            for g in range(PASSES):
-                grouped_words = w_grouped[:, g, :].bitcast(F32)
-                for t0 in range(0, CHUNK_HEADS, 2):
-                    bank = flipped.tile([P, 2, 2, P], F32, name="bank")
-                    for t in range(2):
-                        for w in range(2):
-                            flip(bank[:, t, w, :], w_words, (t0 + t) * WORDS + g * PASS_WORDS + w)
-                    nc.scalar.copy(
-                        out=grouped_words[:, t0 * 2 * P : (t0 + 2) * 2 * P].rearrange(
-                            "p (t r w) -> p t r w", t=2, w=2
-                        ),
-                        in_=bank[:].rearrange("p t w r -> p t r w"),
-                    )
-                nc.vector.quantize_mx(
-                    out=w_codes[:, g, :].bitcast(FP8X4),
-                    scales=w_scales[:, g, :],
-                    in_=w_grouped[:, g, :],
-                )
-            return w_codes, w_scales
+        def new_w(pool):
+            w_grouped = pool.tile([P, PASSES * 4 * CHUNK], BF16, align_bytes=64)
+            w_codes = pool.tile([P, PASSES * CHUNK], U32, align_bytes=64)
+            w_scales = pool.tile([P, PASSES * CHUNK], U8, align_bytes=64)
+            return w_grouped, w_codes, w_scales
 
-        def project(m, w_codes, w_scales):
-            acc = sums.tile([P, CHUNK], F32)
+        def flip_w(w_raw, t, w, copy):
+            words = w[0][:].bitcast(F32).rearrange("p (g c) -> p g c", g=PASSES)
+            flip(w_raw, t, words[:, :, t * 2 * P : (t + 1) * 2 * P], copy)
+
+        def quantize_w(w, g0, g1):
+            nc.vector.quantize_mx(
+                out=w[1][:, g0 * CHUNK : g1 * CHUNK].bitcast(FP8X4),
+                scales=w[2][:, g0 * CHUNK : g1 * CHUNK],
+                in_=w[0][:, g0 * 4 * CHUNK : g1 * 4 * CHUNK],
+            )
+
+        def project(m, w):
+            acc = sums.tile([P, CHUNK], F32, name="acc")
             for g in range(PASSES):
                 x_cols = slice((m * PASSES + g) * P, (m * PASSES + g + 1) * P)
+                w_cols = slice(g * CHUNK, (g + 1) * CHUNK)
                 nc.tensor.matmul_mx(
                     out=acc[:],
                     lhsT=x_codes[:, x_cols].bitcast(FP8X4),
                     lhsT_scale=x_scales[:, x_cols],
-                    rhs=w_codes[:, g, :].bitcast(FP8X4),
-                    rhs_scale=w_scales[:, g, :],
+                    rhs=w[1][:, w_cols].bitcast(FP8X4),
+                    rhs_scale=w[2][:, w_cols],
                     start=(g == 0),
                     stop=(g == PASSES - 1),
                 )
             return acc
 
-        for m in range(ROW_TILES):
-            prepare_x(m)
-        ready = prepare_w(0)
+        def multiply(acc, m, products, i):
+            shape = [P, 2, CHUNK_HEADS, HEAD]
+            nc.vector.tensor_tensor(
+                out=products[:, i],
+                in0=acc[:].rearrange("p (h d) -> p h d", h=CHUNK_HEADS).unsqueeze(1).to_broadcast(shape),
+                in1=factors[:, m].unsqueeze(2).to_broadcast(shape),
+                op=MULT,
+            )
 
-        for c in range(len(chunks)):
-            w_codes, w_scales = ready
-            if c + 1 < len(chunks):
-                ready = prepare_w(c + 1)
-            out_rows, rotated = chunks[c][1], chunks[c][2]
-            for m0 in range(0, ROW_TILES, 2):
-                result = work.tile([P, 2, CHUNK_HEADS, HEAD], F32)
-                if rotated:
-                    products = work.tile([P, 2, 2, CHUNK_HEADS, HEAD], F32)
-                    for i in range(2):
-                        acc = project(m0 + i, w_codes, w_scales)
-                        shape = [P, 2, CHUNK_HEADS, HEAD]
-                        nc.vector.tensor_tensor(
-                            out=products[:, i],
-                            in0=acc[:].rearrange("p (h d) -> p h d", h=CHUNK_HEADS)
-                            .unsqueeze(1).to_broadcast(shape),
-                            in1=factors[:, m0 + i].unsqueeze(2).to_broadcast(shape),
-                            op=MULT,
-                        )
-                    for mine, other in ((slice(0, HALF), slice(HALF, HEAD)), (slice(HALF, HEAD), slice(0, HALF))):
-                        nc.gpsimd.tensor_tensor(
-                            out=result[:, :, :, mine],
-                            in0=products[:, :, 0, :, mine],
-                            in1=products[:, :, 1, :, other],
-                            op=ADD,
-                        )
-                else:
-                    for i in range(2):
-                        acc = project(m0 + i, w_codes, w_scales)
-                        nc.scalar.copy(out=result[:, i].rearrange("p h d -> p (h d)"), in_=acc[:])
-                nc.sync.dma_start(
-                    out=out_rows[:, m0 : m0 + 2, :],
-                    in_=result[:].rearrange("p i h d -> p i (h d)"),
+        def add_and_store(engine, products, rows, m0, m1):
+            n = m1 - m0
+            result = work.tile([P, 2, CHUNK_HEADS, HEAD], F32, name="result")
+            for mine, other in ((slice(0, HALF), slice(HALF, HEAD)), (slice(HALF, HEAD), slice(0, HALF))):
+                engine.tensor_tensor(
+                    out=result[:, 0:n, :, mine],
+                    in0=products[:, 0:n, 0, :, mine],
+                    in1=products[:, 0:n, 1, :, other],
+                    op=ADD,
                 )
+            nc.sync.dma_start(
+                out=rows[:, m0:m1, :], in_=result[:, 0:n].rearrange("p i h d -> p i (h d)")
+            )
+
+        def project_value(m, w):
+            acc = project(m, w)
+            plain = work.tile([P, CHUNK], F32)
+            nc.scalar.copy(out=plain[:], in_=acc[:])
+            nc.sync.dma_start(out=value[1][:, m, :], in_=plain[:])
+
+        flip_x(0)
+        w_now = new_w(quant)
+        quantize_x(0, 1)
+        for t in range(CHUNK_HEADS):
+            flip_w(w_raws[0], t, w_now, nc.vector.tensor_copy if t % 2 == 0 else nc.scalar.copy)
+        flip_x(1)
+        for g in range(PASSES):
+            quantize_w(w_now, g, g + 1)
+        quantize_x(1, 2)
+
+        STEPS = ROW_TILES // 2
+        LAST = len(rotated) - 1
+        w_value = new_w(keep)
+        for c in range(len(rotated)):
+            rows = rotated[c][1]
+            w_next = new_w(quant) if c < LAST else None
+            for s in range(STEPS):
+                m0 = 2 * s
+                products = work.tile([P, 2, 2, CHUNK_HEADS, HEAD], F32)
+                accs = [project(m0 + i, w_now) for i in range(2)]
+                if c == 0 and s + 1 < STEPS:
+                    flip_x(m0 + 2)
+                    flip_x(m0 + 3)
+                if c < LAST and s % 2 == 0:
+                    for t in (s, s + 1):
+                        flip_w(w_raws[c + 1], t, w_next, nc.scalar.copy)
+                if c in (1, 2) and s % 2 == 1:
+                    flip_w(v_raw, 2 * (c - 1) + s // 2, w_value, nc.scalar.copy)
+                multiply(accs[0], m0, products, 0)
+                if c == 0 and s + 1 < STEPS:
+                    quantize_x(m0 + 2, m0 + 4)
+                multiply(accs[1], m0 + 1, products, 1)
+                if c < LAST and s == STEPS - 1:
+                    quantize_w(w_next, 0, PASSES)
+                if c == 2 and s == STEPS - 1:
+                    quantize_w(w_value, 0, PASSES)
+                if c == LAST and s == STEPS - 1:
+                    add_and_store(nc.gpsimd, products[:, 0:1], rows, m0, m0 + 1)
+                    add_and_store(nc.vector, products[:, 1:2], rows, m0 + 1, m0 + 2)
+                else:
+                    add_and_store(nc.gpsimd, products, rows, m0, m0 + 2)
+                if c in (LAST - 1, LAST):
+                    project_value((c - LAST + 1) * STEPS + s, w_value)
+            w_now = w_next

@@ -56,29 +56,33 @@ def tile_groupedqueryattention_pa_kernel(
         def load_x(m0, m1):
             nc.sync.dma_start(out=x_raw[:, m0 * K : m1 * K], in_=x_rows[:, m0 * K : m1 * K])
 
-        def load_w(chunk, parts):
-            w_raw = weights.tile([P, CHUNK_HEADS * K], BF16, name="w_raw")
-            step = CHUNK_HEADS // parts
-            for t0 in range(0, CHUNK_HEADS, step):
-                nc.sync.dma_start(
-                    out=w_raw[:, t0 * K : (t0 + step) * K].rearrange("p (t k) -> p t k", t=step),
-                    in_=chunk[0][t0 * P : (t0 + step) * P, :].rearrange("(t p) k -> p t k", p=P),
-                )
-            return w_raw
+        def new_raw():
+            return weights.tile([P, CHUNK_HEADS * K], BF16, name="w_raw")
+
+        def load_w(w_raw, chunk, t0, t1):
+            nc.sync.dma_start(
+                out=w_raw[:, t0 * K : t1 * K].rearrange("p (t k) -> p t k", t=t1 - t0),
+                in_=chunk[0][t0 * P : t1 * P, :].rearrange("(t p) k -> p t k", p=P),
+            )
 
         cos_raw = keep.tile([P, ROW_TILES, HEAD], BF16)
         sin_raw = keep.tile([P, ROW_TILES, HEAD], BF16)
         load_x(0, 1)
-        w_raws = [load_w(rotated[0], 2)]
+        w_raws = [new_raw()]
+        load_w(w_raws[0], rotated[0], 0, 2)
         nc.sync.dma_start(out=cos_raw[:], in_=cos_tab.rearrange("(p m) d -> p m d", m=ROW_TILES))
         nc.sync.dma_start(out=sin_raw[:], in_=sin_tab.rearrange("(p m) d -> p m d", m=ROW_TILES))
         load_x(1, 2)
+        load_w(w_raws[0], rotated[0], 2, 4)
         for m0 in range(2, ROW_TILES, 2):
             load_x(m0, m0 + 2)
-        for chunk in rotated[1:4]:
-            w_raws.append(load_w(chunk, 1))
-        v_raw = load_w(value, 1)
-        w_raws.append(load_w(rotated[4], 1))
+        for chunk in rotated[1:]:
+            w_raws.append(new_raw())
+        v_raw = new_raw()
+        for c in (1, 2, 3):
+            load_w(w_raws[c], rotated[c], 0, 4)
+        load_w(v_raw, value, 0, 4)
+        load_w(w_raws[4], rotated[4], 0, 4)
 
         factors = keep.tile([P, ROW_TILES, 2, HEAD], F32)
         for tiles in (slice(0, 2), slice(2, ROW_TILES)):
@@ -124,30 +128,32 @@ def tile_groupedqueryattention_pa_kernel(
                 in_=x_grouped[:, m0 * K : m1 * K],
             )
 
-        def new_w(pool):
+        def new_w(pool, parts):
             w_grouped = pool.tile([P, PASSES * 4 * CHUNK], BF16, align_bytes=64)
             w_codes = pool.tile([P, PASSES * CHUNK], U32, align_bytes=64)
             w_scales = pool.tile([P, PASSES * CHUNK], U8, align_bytes=64)
-            return w_grouped, w_codes, w_scales
+            return w_grouped, w_codes, w_scales, CHUNK // parts
 
         def flip_w(w_raw, t, w, copy):
-            words = w[0][:].bitcast(F32).rearrange("p (g c) -> p g c", g=PASSES)
-            flip(w_raw, t, words[:, :, t * 2 * P : (t + 1) * 2 * P], copy)
+            part, column = divmod(t * P, w[3])
+            words = w[0][:].bitcast(F32)[:, part * PASSES * 2 * w[3] : (part + 1) * PASSES * 2 * w[3]]
+            words = words.rearrange("p (g c) -> p g c", g=PASSES)
+            flip(w_raw, t, words[:, :, 2 * column : 2 * (column + P)], copy)
 
-        def quantize_w(w, g0, g1):
+        def quantize_w(w, part):
+            cols = PASSES * w[3]
             nc.vector.quantize_mx(
-                out=w[1][:, g0 * CHUNK : g1 * CHUNK].bitcast(FP8X4),
-                scales=w[2][:, g0 * CHUNK : g1 * CHUNK],
-                in_=w[0][:, g0 * 4 * CHUNK : g1 * 4 * CHUNK],
+                out=w[1][:, part * cols : (part + 1) * cols].bitcast(FP8X4),
+                scales=w[2][:, part * cols : (part + 1) * cols],
+                in_=w[0][:, part * 4 * cols : (part + 1) * 4 * cols],
             )
 
-        def project(m, w):
-            acc = sums.tile([P, CHUNK], F32, name="acc")
+        def project(acc, m, w, part):
             for g in range(PASSES):
                 x_cols = slice((m * PASSES + g) * P, (m * PASSES + g + 1) * P)
-                w_cols = slice(g * CHUNK, (g + 1) * CHUNK)
+                w_cols = slice((part * PASSES + g) * w[3], (part * PASSES + g + 1) * w[3])
                 nc.tensor.matmul_mx(
-                    out=acc[:],
+                    out=acc,
                     lhsT=x_codes[:, x_cols].bitcast(FP8X4),
                     lhsT_scale=x_scales[:, x_cols],
                     rhs=w[1][:, w_cols].bitcast(FP8X4),
@@ -155,78 +161,116 @@ def tile_groupedqueryattention_pa_kernel(
                     start=(g == 0),
                     stop=(g == PASSES - 1),
                 )
+
+        def new_sums():
+            return sums.tile([P, CHUNK], F32, name="acc")
+
+        def project_all(m, w):
+            acc = new_sums()
+            for part in range(CHUNK // w[3]):
+                project(acc[:, part * w[3] : (part + 1) * w[3]], m, w, part)
             return acc
 
-        def multiply(acc, m, products, i):
-            shape = [P, 2, CHUNK_HEADS, HEAD]
+        def multiply(acc, m, products, i, h0=0, h1=CHUNK_HEADS):
+            shape = [P, 2, h1 - h0, HEAD]
             nc.vector.tensor_tensor(
-                out=products[:, i],
-                in0=acc[:].rearrange("p (h d) -> p h d", h=CHUNK_HEADS).unsqueeze(1).to_broadcast(shape),
+                out=products[:, :, i, h0:h1],
+                in0=acc.rearrange("p (h d) -> p h d", d=HEAD).unsqueeze(1).to_broadcast(shape),
                 in1=factors[:, m].unsqueeze(2).to_broadcast(shape),
                 op=MULT,
             )
 
-        def add_and_store(engine, products, rows, m0, m1):
-            n = m1 - m0
-            result = work.tile([P, 2, CHUNK_HEADS, HEAD], F32, name="result")
-            for mine, other in ((slice(0, HALF), slice(HALF, HEAD)), (slice(HALF, HEAD), slice(0, HALF))):
-                engine.tensor_tensor(
-                    out=result[:, 0:n, :, mine],
-                    in0=products[:, 0:n, 0, :, mine],
-                    in1=products[:, 0:n, 1, :, other],
-                    op=ADD,
-                )
+        def add(engine, products, result, u0, u1):
+            straight = products[:, 0].rearrange("p i h d -> p (i h) d")
+            crossed = products[:, 1].rearrange("p i h (two d) -> p (i h) two d", two=2)
+            engine.tensor_tensor(
+                out=result[:].rearrange("p i h (two d) -> p (i h) two d", two=2)[:, u0:u1],
+                in0=straight.rearrange("p u (two d) -> p u two d", two=2)[:, u0:u1],
+                in1=crossed[:, u0:u1, ::-1, :],
+                op=ADD,
+            )
+
+        def store(result, rows, m0, i0, i1):
             nc.sync.dma_start(
-                out=rows[:, m0:m1, :], in_=result[:, 0:n].rearrange("p i h d -> p i (h d)")
+                out=rows[:, m0 + i0 : m0 + i1, :], in_=result[:, i0:i1].rearrange("p i h d -> p i (h d)")
             )
 
         def project_value(m, w):
-            acc = project(m, w)
+            acc = project_all(m, w)
             plain = work.tile([P, CHUNK], F32)
             nc.scalar.copy(out=plain[:], in_=acc[:])
             nc.sync.dma_start(out=value[1][:, m, :], in_=plain[:])
 
-        flip_x(0)
-        w_now = new_w(quant)
-        quantize_x(0, 1)
-        for t in range(CHUNK_HEADS):
-            flip_w(w_raws[0], t, w_now, nc.vector.tensor_copy if t % 2 == 0 else nc.scalar.copy)
-        flip_x(1)
-        for g in range(PASSES):
-            quantize_w(w_now, g, g + 1)
-        quantize_x(1, 2)
-
         STEPS = ROW_TILES // 2
         LAST = len(rotated) - 1
-        w_value = new_w(keep)
+        UNITS = 2 * CHUNK_HEADS
+        GPSIMD_UNITS = 6
+
+        def new_products():
+            return work.tile([P, 2, 2, CHUNK_HEADS, HEAD], F32, name="products")
+
+        w_now = new_w(quant, 2)
+        flip_x(0)
+        flip_w(w_raws[0], 0, w_now, nc.vector.tensor_copy)
+        flip_w(w_raws[0], 1, w_now, nc.scalar.copy)
+        quantize_x(0, 1)
+        flip_x(1)
+        quantize_w(w_now, 0)
+        flip_w(w_raws[0], 2, w_now, nc.vector.tensor_copy)
+        flip_w(w_raws[0], 3, w_now, nc.scalar.copy)
+        quantize_x(1, 2)
+        products = new_products()
+        for part in range(2):
+            heads = slice(part * CHUNK_HEADS // 2, (part + 1) * CHUNK_HEADS // 2)
+            for i in range(2):
+                acc = new_sums()
+                project(acc[:, : CHUNK // 2], i, w_now, part)
+                multiply(acc[:, : CHUNK // 2], i, products, i, heads.start, heads.stop)
+                if (part, i) == (0, 0):
+                    quantize_w(w_now, 1)
+        flip_x(2)
+        flip_x(3)
+        quantize_x(2, 4)
+
+        w_value = new_w(keep, 1)
+        behind = None
         for c in range(len(rotated)):
             rows = rotated[c][1]
-            w_next = new_w(quant) if c < LAST else None
+            w_next = new_w(quant, 1) if c < LAST else None
             for s in range(STEPS):
                 m0 = 2 * s
-                products = work.tile([P, 2, 2, CHUNK_HEADS, HEAD], F32)
-                accs = [project(m0 + i, w_now) for i in range(2)]
-                if c == 0 and s + 1 < STEPS:
-                    flip_x(m0 + 2)
-                    flip_x(m0 + 3)
-                if c < LAST and s % 2 == 0:
-                    for t in (s, s + 1):
+                result = work.tile([P, 2, CHUNK_HEADS, HEAD], F32)
+                if (c, s) != (0, 0):
+                    products = new_products()
+                    accs = [project_all(m0 + i, w_now) for i in range(2)]
+                if c == 0 and s + 2 < STEPS:
+                    flip_x(m0 + 4)
+                    flip_x(m0 + 5)
+                if c < LAST and s < 2:
+                    for t in (2 * s, 2 * s + 1):
                         flip_w(w_raws[c + 1], t, w_next, nc.scalar.copy)
-                if c in (1, 2) and s % 2 == 1:
-                    flip_w(v_raw, 2 * (c - 1) + s // 2, w_value, nc.scalar.copy)
-                multiply(accs[0], m0, products, 0)
-                if c == 0 and s + 1 < STEPS:
-                    quantize_x(m0 + 2, m0 + 4)
-                multiply(accs[1], m0 + 1, products, 1)
-                if c < LAST and s == STEPS - 1:
-                    quantize_w(w_next, 0, PASSES)
-                if c == 2 and s == STEPS - 1:
-                    quantize_w(w_value, 0, PASSES)
+                if c in (1, 2) and s == 2:
+                    for t in (2 * c - 2, 2 * c - 1):
+                        flip_w(v_raw, t, w_value, nc.scalar.copy)
+                if (c, s) != (0, 0):
+                    multiply(accs[0][:], m0, products, 0)
+                    multiply(accs[1][:], m0 + 1, products, 1)
+                if c == 0 and s + 2 < STEPS:
+                    quantize_x(m0 + 4, m0 + 6)
+                if behind is not None:
+                    add(nc.vector, behind[0], behind[1], GPSIMD_UNITS, UNITS)
+                    store(behind[1], behind[2], behind[3], 0, 2)
+                if c < LAST and s == 2:
+                    quantize_w(w_next, 0)
+                if c == 2 and s == 3:
+                    quantize_w(w_value, 0)
                 if c == LAST and s == STEPS - 1:
-                    add_and_store(nc.gpsimd, products[:, 0:1], rows, m0, m0 + 1)
-                    add_and_store(nc.vector, products[:, 1:2], rows, m0 + 1, m0 + 2)
+                    for i in range(2):
+                        add(nc.vector, products, result, i * CHUNK_HEADS, (i + 1) * CHUNK_HEADS)
+                        store(result, rows, m0, i, i + 1)
                 else:
-                    add_and_store(nc.gpsimd, products, rows, m0, m0 + 2)
+                    add(nc.gpsimd, products, result, 0, GPSIMD_UNITS)
+                    behind = (products, result, rows, m0)
                 if c in (LAST - 1, LAST):
                     project_value((c - LAST + 1) * STEPS + s, w_value)
             w_now = w_next

@@ -67,13 +67,21 @@ def tile_groupedqueryattention_pa_kernel(
 
         cos_raw = keep.tile([P, ROW_TILES, HEAD], BF16)
         sin_raw = keep.tile([P, ROW_TILES, HEAD], BF16)
+        def load_tables(m0, m1):
+            for raw, table in ((cos_raw, cos_tab), (sin_raw, sin_tab)):
+                nc.sync.dma_start(
+                    out=raw[:, m0:m1, :],
+                    in_=table.rearrange("(p m) d -> p m d", m=ROW_TILES)[:, m0:m1, :],
+                )
+
         load_x(0, 1)
         w_raws = [new_raw()]
-        load_w(w_raws[0], rotated[0], 0, 2)
-        nc.sync.dma_start(out=cos_raw[:], in_=cos_tab.rearrange("(p m) d -> p m d", m=ROW_TILES))
-        nc.sync.dma_start(out=sin_raw[:], in_=sin_tab.rearrange("(p m) d -> p m d", m=ROW_TILES))
+        load_w(w_raws[0], rotated[0], 0, 1)
+        load_w(w_raws[0], rotated[0], 1, 2)
+        load_tables(0, 2)
         load_x(1, 2)
         load_w(w_raws[0], rotated[0], 2, 4)
+        load_tables(2, ROW_TILES)
         for m0 in range(2, ROW_TILES, 2):
             load_x(m0, m0 + 2)
         for chunk in rotated[1:]:
@@ -206,6 +214,10 @@ def tile_groupedqueryattention_pa_kernel(
         UNITS = 2 * CHUNK_HEADS
         GPSIMD_UNITS = 6
 
+        QUANTISING = ((0, 1), (0, 2), (1, 2), (2, 2), (2, 3), (3, 2))
+        FLIPS = ((0, 1), (2, 3), (), ())
+        FLIPS_FIRST = ((), (0,), (1, 2, 3), ())
+
         def new_products():
             return work.tile([P, 2, 2, CHUNK_HEADS, HEAD], F32, name="products")
 
@@ -216,21 +228,23 @@ def tile_groupedqueryattention_pa_kernel(
         quantize_x(0, 1)
         flip_x(1)
         quantize_w(w_now, 0)
-        flip_w(w_raws[0], 2, w_now, nc.vector.tensor_copy)
-        flip_w(w_raws[0], 3, w_now, nc.scalar.copy)
         quantize_x(1, 2)
+        flip_w(w_raws[0], 2, w_now, nc.vector.tensor_copy)
         products = new_products()
         for part in range(2):
-            heads = slice(part * CHUNK_HEADS // 2, (part + 1) * CHUNK_HEADS // 2)
+            h0, h1 = part * CHUNK_HEADS // 2, (part + 1) * CHUNK_HEADS // 2
+            accs = [new_sums()[:, : CHUNK // 2] for i in range(2)]
             for i in range(2):
-                acc = new_sums()
-                project(acc[:, : CHUNK // 2], i, w_now, part)
-                multiply(acc[:, : CHUNK // 2], i, products, i, heads.start, heads.stop)
-                if (part, i) == (0, 0):
-                    quantize_w(w_now, 1)
-        flip_x(2)
-        flip_x(3)
-        quantize_x(2, 4)
+                project(accs[i], i, w_now, part)
+            if part == 0:
+                flip_w(w_raws[0], 3, w_now, nc.scalar.copy)
+                flip_x(2)
+                flip_x(3)
+            multiply(accs[0], 0, products, 0, h0, h1)
+            multiply(accs[1], 1, products, 1, h0, h1)
+            if part == 0:
+                quantize_w(w_now, 1)
+                quantize_x(2, 4)
 
         w_value = new_w(keep, 1)
         behind = None
@@ -246,8 +260,8 @@ def tile_groupedqueryattention_pa_kernel(
                 if c == 0 and s + 2 < STEPS:
                     flip_x(m0 + 4)
                     flip_x(m0 + 5)
-                if c < LAST and s < 2:
-                    for t in (2 * s, 2 * s + 1):
+                if c < LAST:
+                    for t in FLIPS_FIRST[s] if c == 0 else FLIPS[s]:
                         flip_w(w_raws[c + 1], t, w_next, nc.scalar.copy)
                 if c in (1, 2) and s == 2:
                     for t in (2 * c - 2, 2 * c - 1):
@@ -260,6 +274,7 @@ def tile_groupedqueryattention_pa_kernel(
                 if behind is not None:
                     add(nc.vector, behind[0], behind[1], GPSIMD_UNITS, UNITS)
                     store(behind[1], behind[2], behind[3], 0, 2)
+                    behind = None
                 if c < LAST and s == 2:
                     quantize_w(w_next, 0)
                 if c == 2 and s == 3:
@@ -268,6 +283,9 @@ def tile_groupedqueryattention_pa_kernel(
                     for i in range(2):
                         add(nc.vector, products, result, i * CHUNK_HEADS, (i + 1) * CHUNK_HEADS)
                         store(result, rows, m0, i, i + 1)
+                elif (c, s + 1) in QUANTISING:
+                    add(nc.gpsimd, products, result, 0, UNITS)
+                    store(result, rows, m0, 0, 2)
                 else:
                     add(nc.gpsimd, products, result, 0, GPSIMD_UNITS)
                     behind = (products, result, rows, m0)

@@ -212,9 +212,9 @@ def tile_groupedqueryattention_pa_kernel(
         STEPS = ROW_TILES // 2
         LAST = len(rotated) - 1
         UNITS = 2 * CHUNK_HEADS
-        GPSIMD_UNITS = 6
+        GPSIMD_UNITS = 7
 
-        QUANTISING = ((0, 1), (0, 2), (1, 2), (2, 2), (2, 3), (3, 2))
+        QUANTISING = ((0, 1), (0, 2), (1, 1), (1, 3), (2, 1), (3, 1), (LAST, STEPS - 1))
         FLIPS = ((0, 1), (2, 3), (), ())
         FLIPS_FIRST = ((), (0,), (1, 2, 3), ())
 
@@ -263,8 +263,8 @@ def tile_groupedqueryattention_pa_kernel(
                 if c < LAST:
                     for t in FLIPS_FIRST[s] if c == 0 else FLIPS[s]:
                         flip_w(w_raws[c + 1], t, w_next, nc.scalar.copy)
-                if c in (1, 2) and s == 2:
-                    for t in (2 * c - 2, 2 * c - 1):
+                if c == 1 and s >= 2:
+                    for t in (2 * s - 4, 2 * s - 3):
                         flip_w(v_raw, t, w_value, nc.scalar.copy)
                 if (c, s) != (0, 0):
                     multiply(accs[0][:], m0, products, 0)
@@ -275,9 +275,9 @@ def tile_groupedqueryattention_pa_kernel(
                     add(nc.vector, behind[0], behind[1], GPSIMD_UNITS, UNITS)
                     store(behind[1], behind[2], behind[3], 0, 2)
                     behind = None
-                if c < LAST and s == 2:
+                if c < LAST and s == (2 if c == 0 else 1):
                     quantize_w(w_next, 0)
-                if c == 2 and s == 3:
+                if c == 1 and s == 3:
                     quantize_w(w_value, 0)
                 if c == LAST and s == STEPS - 1:
                     for i in range(2):

@@ -221,12 +221,24 @@ def tile_groupedqueryattention_pa_kernel(
         def new_products():
             return work.tile([P, 2, 2, CHUNK_HEADS, HEAD], F32, name="products")
 
+        zeros = keep.tile([P, CHUNK], BF16)
+        nc.vector.memset(zeros[:], 0.0)
+        idle_sums = new_sums()
+
+        def warm(times):
+            for i in range(times):
+                nc.tensor.matmul(idle_sums[:], lhsT=zeros[:, :P], rhs=zeros[:], start=True, stop=True)
+
         w_now = new_w(quant, 2)
+        warm(5)
         flip_x(0)
+        warm(1)
         flip_w(w_raws[0], 0, w_now, nc.vector.tensor_copy)
         flip_w(w_raws[0], 1, w_now, nc.scalar.copy)
+        warm(1)
         quantize_x(0, 1)
         flip_x(1)
+        warm(1)
         quantize_w(w_now, 0)
         quantize_x(1, 2)
         flip_w(w_raws[0], 2, w_now, nc.vector.tensor_copy)

@@ -44,7 +44,7 @@ def tile_groupedqueryattention_pa_kernel(
         name="weights", bufs=len(rotated) + 1
     ) as weights, tc.tile_pool(name="quant", bufs=2) as quant, tc.tile_pool(
         name="work", bufs=4
-    ) as work, tc.psum_pool(name="flipped", bufs=4) as flipped, tc.psum_pool(
+    ) as work, tc.tile_pool(name="order", bufs=6) as order, tc.psum_pool(name="flipped", bufs=4) as flipped, tc.psum_pool(
         name="sums", bufs=4
     ) as sums, tc.manual_schedule():
         identity = keep.tile([P, P], F32)
@@ -107,19 +107,24 @@ def tile_groupedqueryattention_pa_kernel(
                 scalar1=-1.0, scalar2=0.0, op0=MULT, op1=ADD,
             )
 
-        def flip(raw, tile, grouped, copy):
+        def flip(planes, grouped, copy):
             bank = flipped.tile([P, PASSES, 2, P], F32, name="bank")
-            words = raw[:].bitcast(F32)
             for g in range(PASSES):
                 for w in range(2):
-                    first = tile * PAIRS + g * PASS_PAIRS + w
-                    nc.tensor.transpose(
-                        bank[:, g, w, :], words[:, first : first + PASS_PAIRS - 1 : 2], identity[:]
-                    )
+                    nc.tensor.transpose(bank[:, g, w, :], planes[:, g, w, :], identity[:])
             copy(
                 out=grouped.rearrange("p g (r w) -> p g r w", w=2),
                 in_=bank[:].rearrange("p g w r -> p g r w"),
             )
+
+        def planes_of(raw, tile):
+            words = raw[:].bitcast(F32)[:, tile * PAIRS : (tile + 1) * PAIRS]
+            return words.rearrange("p (g r w) -> p g w r", g=PASSES, w=2)
+
+        def ordered(raw, tile):
+            words = order.tile([P, PASSES, 2, P], F32, name="words")
+            nc.scalar.copy(out=words[:], in_=planes_of(raw, tile))
+            return words[:]
 
         x_grouped = keep.tile([P, ROW_TILES * K], BF16, align_bytes=64)
         x_codes = keep.tile([P, ROW_TILES * K // 4], U32, align_bytes=64)
@@ -127,7 +132,7 @@ def tile_groupedqueryattention_pa_kernel(
 
         def flip_x(m):
             words = x_grouped[:].bitcast(F32)[:, m * PAIRS : (m + 1) * PAIRS]
-            flip(x_raw, m, words.rearrange("p (g c) -> p g c", g=PASSES), nc.scalar.copy)
+            flip(planes_of(x_raw, m), words.rearrange("p (g c) -> p g c", g=PASSES), nc.scalar.copy)
 
         def quantize_x(m0, m1):
             nc.vector.quantize_mx(
@@ -142,11 +147,11 @@ def tile_groupedqueryattention_pa_kernel(
             w_scales = pool.tile([P, PASSES * CHUNK], U8, align_bytes=64)
             return w_grouped, w_codes, w_scales, CHUNK // parts
 
-        def flip_w(w_raw, t, w, copy):
+        def flip_w(planes, t, w, copy):
             part, column = divmod(t * P, w[3])
             words = w[0][:].bitcast(F32)[:, part * PASSES * 2 * w[3] : (part + 1) * PASSES * 2 * w[3]]
             words = words.rearrange("p (g c) -> p g c", g=PASSES)
-            flip(w_raw, t, words[:, :, 2 * column : 2 * (column + P)], copy)
+            flip(planes, words[:, :, 2 * column : 2 * (column + P)], copy)
 
         def quantize_w(w, part):
             cols = PASSES * w[3]
@@ -218,6 +223,14 @@ def tile_groupedqueryattention_pa_kernel(
         FLIPS = ((0, 1), (2, 3), (), ())
         FLIPS_FIRST = ((), (0,), (1, 2, 3), ())
 
+        def tiles_to_turn(c, s):
+            tiles = []
+            if c < LAST:
+                tiles += [(w_raws[c + 1], t) for t in (FLIPS_FIRST[s] if c == 0 else FLIPS[s])]
+            if c == 1 and s >= 2:
+                tiles += [(v_raw, 2 * s - 4), (v_raw, 2 * s - 3)]
+            return tiles
+
         def new_products():
             return work.tile([P, 2, 2, CHUNK_HEADS, HEAD], F32, name="products")
 
@@ -233,15 +246,15 @@ def tile_groupedqueryattention_pa_kernel(
         warm(5)
         flip_x(0)
         warm(1)
-        flip_w(w_raws[0], 0, w_now, nc.vector.tensor_copy)
-        flip_w(w_raws[0], 1, w_now, nc.scalar.copy)
+        flip_w(planes_of(w_raws[0], 0), 0, w_now, nc.vector.tensor_copy)
+        flip_w(planes_of(w_raws[0], 1), 1, w_now, nc.scalar.copy)
         warm(1)
         quantize_x(0, 1)
         flip_x(1)
         warm(1)
         quantize_w(w_now, 0)
         quantize_x(1, 2)
-        flip_w(w_raws[0], 2, w_now, nc.vector.tensor_copy)
+        flip_w(planes_of(w_raws[0], 2), 2, w_now, nc.vector.tensor_copy)
         products = new_products()
         for part in range(2):
             h0, h1 = part * CHUNK_HEADS // 2, (part + 1) * CHUNK_HEADS // 2
@@ -249,7 +262,7 @@ def tile_groupedqueryattention_pa_kernel(
             for i in range(2):
                 project(accs[i], i, w_now, part)
             if part == 0:
-                flip_w(w_raws[0], 3, w_now, nc.scalar.copy)
+                flip_w(planes_of(w_raws[0], 3), 3, w_now, nc.scalar.copy)
                 flip_x(2)
                 flip_x(3)
             multiply(accs[0], 0, products, 0, h0, h1)
@@ -259,6 +272,7 @@ def tile_groupedqueryattention_pa_kernel(
                 quantize_x(2, 4)
 
         w_value = new_w(keep, 1)
+        planes_ahead = {}
         behind = None
         for c in range(len(rotated)):
             rows = rotated[c][1]
@@ -268,19 +282,20 @@ def tile_groupedqueryattention_pa_kernel(
                 result = work.tile([P, 2, CHUNK_HEADS, HEAD], F32)
                 if (c, s) != (0, 0):
                     products = new_products()
-                    accs = [project_all(m0 + i, w_now) for i in range(2)]
+                turns = []
                 if c == 0 and s + 2 < STEPS:
-                    flip_x(m0 + 4)
-                    flip_x(m0 + 5)
-                if c < LAST:
-                    for t in FLIPS_FIRST[s] if c == 0 else FLIPS[s]:
-                        flip_w(w_raws[c + 1], t, w_next, nc.scalar.copy)
-                if c == 1 and s >= 2:
-                    for t in (2 * s - 4, 2 * s - 3):
-                        flip_w(v_raw, t, w_value, nc.scalar.copy)
-                if (c, s) != (0, 0):
-                    multiply(accs[0][:], m0, products, 0)
-                    multiply(accs[1][:], m0 + 1, products, 1)
+                    turns += [(flip_x, (m0 + 4,)), (flip_x, (m0 + 5,))]
+                for n, (raw, t) in enumerate(tiles_to_turn(c, s)):
+                    planes = planes_of(raw, t) if c == 0 else planes_ahead[(c, s)][n]
+                    turns.append((flip_w, (planes, t, w_value if raw is v_raw else w_next, nc.scalar.copy)))
+                later = divmod(c * STEPS + s + 2, STEPS)
+                if later[0] > 0:
+                    planes_ahead[later] = [ordered(raw, t) for raw, t in tiles_to_turn(later[0], later[1])]
+                for i in range(2):
+                    if (c, s) != (0, 0):
+                        multiply(project_all(m0 + i, w_now)[:], m0 + i, products, i)
+                    for turn, operands in turns[: len(turns) // 2] if i == 0 else turns[len(turns) // 2 :]:
+                        turn(*operands)
                 if c == 0 and s + 2 < STEPS:
                     quantize_x(m0 + 4, m0 + 6)
                 if behind is not None:

@@ -44,7 +44,9 @@ def tile_groupedqueryattention_pa_kernel(
         name="weights", bufs=len(rotated) + 1
     ) as weights, tc.tile_pool(name="quant", bufs=2) as quant, tc.tile_pool(
         name="work", bufs=4
-    ) as work, tc.tile_pool(name="order", bufs=6) as order, tc.psum_pool(name="flipped", bufs=4) as flipped, tc.psum_pool(
+    ) as work, tc.tile_pool(name="order", bufs=6) as order, tc.tile_pool(
+        name="values", bufs=ROW_TILES
+    ) as values, tc.psum_pool(name="flipped", bufs=4) as flipped, tc.psum_pool(
         name="sums", bufs=4
     ) as sums, tc.manual_schedule():
         identity = keep.tile([P, P], F32)
@@ -210,7 +212,7 @@ def tile_groupedqueryattention_pa_kernel(
 
         def project_value(m, w):
             acc = project_all(m, w)
-            plain = work.tile([P, CHUNK], F32)
+            plain = values.tile([P, CHUNK], F32)
             nc.scalar.copy(out=plain[:], in_=acc[:])
             nc.sync.dma_start(out=value[1][:, m, :], in_=plain[:])
 
@@ -219,6 +221,7 @@ def tile_groupedqueryattention_pa_kernel(
         UNITS = 2 * CHUNK_HEADS
         GPSIMD_UNITS = 7
 
+        VALUE_STEPS = ((2, 2), (2, 3), (3, 2), (3, 3))
         QUANTISING = ((0, 1), (0, 2), (1, 1), (1, 3), (2, 1), (3, 1), (LAST, STEPS - 1))
         FLIPS = ((0, 1), (2, 3), (), ())
         FLIPS_FIRST = ((), (0,), (1, 2, 3), ())
@@ -263,8 +266,8 @@ def tile_groupedqueryattention_pa_kernel(
                 project(accs[i], i, w_now, part)
             if part == 0:
                 flip_w(planes_of(w_raws[0], 3), 3, w_now, nc.scalar.copy)
-                flip_x(2)
-                flip_x(3)
+                for m in range(2, 5):
+                    flip_x(m)
             multiply(accs[0], 0, products, 0, h0, h1)
             multiply(accs[1], 1, products, 1, h0, h1)
             if part == 0:
@@ -284,7 +287,7 @@ def tile_groupedqueryattention_pa_kernel(
                     products = new_products()
                 turns = []
                 if c == 0 and s + 2 < STEPS:
-                    turns += [(flip_x, (m0 + 4,)), (flip_x, (m0 + 5,))]
+                    turns += [(flip_x, (m,)) for m in range(5 if s == 0 else m0 + 4, m0 + 6)]
                 for n, (raw, t) in enumerate(tiles_to_turn(c, s)):
                     planes = planes_of(raw, t) if c == 0 else planes_ahead[(c, s)][n]
                     turns.append((flip_w, (planes, t, w_value if raw is v_raw else w_next, nc.scalar.copy)))
@@ -316,6 +319,7 @@ def tile_groupedqueryattention_pa_kernel(
                 else:
                     add(nc.gpsimd, products, result, 0, GPSIMD_UNITS)
                     behind = (products, result, rows, m0)
-                if c in (LAST - 1, LAST):
-                    project_value((c - LAST + 1) * STEPS + s, w_value)
+                if (c, s) in VALUE_STEPS:
+                    for i in range(2):
+                        project_value(2 * VALUE_STEPS.index((c, s)) + i, w_value)
             w_now = w_next

import concourse.mybir as mybir
from concourse.masks import make_identity

F32 = mybir.dt.float32
BF16 = mybir.dt.bfloat16
U32 = mybir.dt.uint32
U8 = mybir.dt.uint8
FP8X4 = mybir.dt.float8_e4m3fn_x4
MULT = mybir.AluOpType.mult
ADD = mybir.AluOpType.add

P = 128
ROWS = 1024
K = 1024
HEAD = 128
HALF = HEAD // 2
K_PASS = 4 * P
PASSES = K // K_PASS
PAIRS = K // 2
PASS_PAIRS = K_PASS // 2
ROW_TILES = ROWS // P
CHUNK_HEADS = 4
CHUNK = CHUNK_HEADS * HEAD

FLOPS = 2 * ROWS * K * (2048 + 512 + 512)


def tile_groupedqueryattention_pa_kernel(
    tc, x, w_q, w_k, w_v, cos_tab, sin_tab, out_0, out_1, out_2
):
    nc = tc.nc

    def rows_on_partitions(out):
        return out.rearrange("(p m) h d -> p m (h d)", m=ROW_TILES)

    rotated = []
    for c in range(w_q.shape[0] // CHUNK):
        cols = slice(c * CHUNK, (c + 1) * CHUNK)
        rotated.append((w_q[cols, :], rows_on_partitions(out_0)[:, :, cols]))
    rotated.append((w_k, rows_on_partitions(out_1)))
    value = (w_v, rows_on_partitions(out_2))

    with tc.tile_pool(name="keep", bufs=1) as keep, tc.tile_pool(
        name="weights", bufs=len(rotated) + 1
    ) as weights, tc.tile_pool(name="quant", bufs=2) as quant, tc.tile_pool(
        name="work", bufs=4
    ) as work, tc.tile_pool(name="order", bufs=6) as order, tc.tile_pool(
        name="values", bufs=ROW_TILES
    ) as values, tc.psum_pool(name="flipped", bufs=4) as flipped, tc.psum_pool(
        name="sums", bufs=4
    ) as sums, tc.manual_schedule():
        identity = keep.tile([P, P], F32)
        make_identity(nc, identity[:])

        x_raw = keep.tile([P, ROW_TILES * K], BF16)
        x_rows = x.rearrange("(p m) k -> p (m k)", m=ROW_TILES)

        def load_x(m0, m1):
            nc.sync.dma_start(out=x_raw[:, m0 * K : m1 * K], in_=x_rows[:, m0 * K : m1 * K])

        def new_raw():
            return weights.tile([P, CHUNK_HEADS * K], BF16, name="w_raw")

        def load_w(w_raw, chunk, t0, t1):
            nc.sync.dma_start(
                out=w_raw[:, t0 * K : t1 * K].rearrange("p (t k) -> p t k", t=t1 - t0),
                in_=chunk[0][t0 * P : t1 * P, :].rearrange("(t p) k -> p t k", p=P),
            )

        cos_raw = keep.tile([P, ROW_TILES, HEAD], BF16)
        sin_raw = keep.tile([P, ROW_TILES, HEAD], BF16)
        def load_tables(m0, m1):
            for raw, table in ((cos_raw, cos_tab), (sin_raw, sin_tab)):
                nc.sync.dma_start(
                    out=raw[:, m0:m1, :],
                    in_=table.rearrange("(p m) d -> p m d", m=ROW_TILES)[:, m0:m1, :],
                )

        load_x(0, 1)
        w_raws = [new_raw()]
        load_w(w_raws[0], rotated[0], 0, 1)
        load_w(w_raws[0], rotated[0], 1, 2)
        load_tables(0, 2)
        load_x(1, 2)
        load_w(w_raws[0], rotated[0], 2, 4)
        load_tables(2, ROW_TILES)
        for m0 in range(2, ROW_TILES, 2):
            load_x(m0, m0 + 2)
        for chunk in rotated[1:]:
            w_raws.append(new_raw())
        v_raw = new_raw()
        for c in (1, 2, 3):
            load_w(w_raws[c], rotated[c], 0, 4)
        load_w(v_raw, value, 0, 4)
        load_w(w_raws[4], rotated[4], 0, 4)

        factors = keep.tile([P, ROW_TILES, 2, HEAD], F32)
        for tiles in (slice(0, 2), slice(2, ROW_TILES)):
            nc.gpsimd.tensor_scalar(
                out=factors[:, tiles, 0, :], in0=cos_raw[:, tiles, :],
                scalar1=1.0, scalar2=0.0, op0=MULT, op1=ADD,
            )
            nc.gpsimd.tensor_scalar(
                out=factors[:, tiles, 1, 0:HALF], in0=sin_raw[:, tiles, HALF:HEAD],
                scalar1=1.0, scalar2=0.0, op0=MULT, op1=ADD,
            )
            nc.gpsimd.tensor_scalar(
                out=factors[:, tiles, 1, HALF:HEAD], in0=sin_raw[:, tiles, 0:HALF],
                scalar1=-1.0, scalar2=0.0, op0=MULT, op1=ADD,
            )

        def flip(planes, grouped, copy):
            bank = flipped.tile([P, PASSES, 2, P], F32, name="bank")
            for g in range(PASSES):
                for w in range(2):
                    nc.tensor.transpose(bank[:, g, w, :], planes[:, g, w, :], identity[:])
            copy(
                out=grouped.rearrange("p g (r w) -> p g r w", w=2),
                in_=bank[:].rearrange("p g w r -> p g r w"),
            )

        def planes_of(raw, tile):
            words = raw[:].bitcast(F32)[:, tile * PAIRS : (tile + 1) * PAIRS]
            return words.rearrange("p (g r w) -> p g w r", g=PASSES, w=2)

        def ordered(raw, tile):
            words = order.tile([P, PASSES, 2, P], F32, name="words")
            nc.scalar.copy(out=words[:], in_=planes_of(raw, tile))
            return words[:]

        x_grouped = keep.tile([P, ROW_TILES * K], BF16, align_bytes=64)
        x_codes = keep.tile([P, ROW_TILES * K // 4], U32, align_bytes=64)
        x_scales = keep.tile([P, ROW_TILES * K // 4], U8, align_bytes=64)

        def flip_x(m):
            words = x_grouped[:].bitcast(F32)[:, m * PAIRS : (m + 1) * PAIRS]
            flip(planes_of(x_raw, m), words.rearrange("p (g c) -> p g c", g=PASSES), nc.scalar.copy)

        def quantize_x(m0, m1):
            nc.vector.quantize_mx(
                out=x_codes[:, m0 * K // 4 : m1 * K // 4].bitcast(FP8X4),
                scales=x_scales[:, m0 * K // 4 : m1 * K // 4],
                in_=x_grouped[:, m0 * K : m1 * K],
            )

        def new_w(pool, parts):
            w_grouped = pool.tile([P, PASSES * 4 * CHUNK], BF16, align_bytes=64)
            w_codes = pool.tile([P, PASSES * CHUNK], U32, align_bytes=64)
            w_scales = pool.tile([P, PASSES * CHUNK], U8, align_bytes=64)
            return w_grouped, w_codes, w_scales, CHUNK // parts

        def flip_w(planes, t, w, copy):
            part, column = divmod(t * P, w[3])
            words = w[0][:].bitcast(F32)[:, part * PASSES * 2 * w[3] : (part + 1) * PASSES * 2 * w[3]]
            words = words.rearrange("p (g c) -> p g c", g=PASSES)
            flip(planes, words[:, :, 2 * column : 2 * (column + P)], copy)

        def quantize_w(w, part):
            cols = PASSES * w[3]
            nc.vector.quantize_mx(
                out=w[1][:, part * cols : (part + 1) * cols].bitcast(FP8X4),
                scales=w[2][:, part * cols : (part + 1) * cols],
                in_=w[0][:, part * 4 * cols : (part + 1) * 4 * cols],
            )

        def project(acc, m, w, part):
            for g in range(PASSES):
                x_cols = slice((m * PASSES + g) * P, (m * PASSES + g + 1) * P)
                w_cols = slice((part * PASSES + g) * w[3], (part * PASSES + g + 1) * w[3])
                nc.tensor.matmul_mx(
                    out=acc,
                    lhsT=x_codes[:, x_cols].bitcast(FP8X4),
                    lhsT_scale=x_scales[:, x_cols],
                    rhs=w[1][:, w_cols].bitcast(FP8X4),
                    rhs_scale=w[2][:, w_cols],
                    start=(g == 0),
                    stop=(g == PASSES - 1),
                )

        def new_sums():
            return sums.tile([P, CHUNK], F32, name="acc")

        def project_all(m, w):
            acc = new_sums()
            for part in range(CHUNK // w[3]):
                project(acc[:, part * w[3] : (part + 1) * w[3]], m, w, part)
            return acc

        def multiply(acc, m, products, i, h0=0, h1=CHUNK_HEADS):
            shape = [P, 2, h1 - h0, HEAD]
            nc.vector.tensor_tensor(
                out=products[:, :, i, h0:h1],
                in0=acc.rearrange("p (h d) -> p h d", d=HEAD).unsqueeze(1).to_broadcast(shape),
                in1=factors[:, m].unsqueeze(2).to_broadcast(shape),
                op=MULT,
            )

        def add(engine, products, result, u0, u1):
            straight = products[:, 0].rearrange("p i h d -> p (i h) d")
            crossed = products[:, 1].rearrange("p i h (two d) -> p (i h) two d", two=2)
            engine.tensor_tensor(
                out=result[:].rearrange("p i h (two d) -> p (i h) two d", two=2)[:, u0:u1],
                in0=straight.rearrange("p u (two d) -> p u two d", two=2)[:, u0:u1],
                in1=crossed[:, u0:u1, ::-1, :],
                op=ADD,
            )

        def store(result, rows, m0, i0, i1):
            nc.sync.dma_start(
                out=rows[:, m0 + i0 : m0 + i1, :], in_=result[:, i0:i1].rearrange("p i h d -> p i (h d)")
            )

        def project_value(m, w):
            acc = project_all(m, w)
            plain = values.tile([P, CHUNK], F32)
            nc.scalar.copy(out=plain[:], in_=acc[:])
            nc.sync.dma_start(out=value[1][:, m, :], in_=plain[:])

        STEPS = ROW_TILES // 2
        LAST = len(rotated) - 1
        UNITS = 2 * CHUNK_HEADS
        GPSIMD_UNITS = 7

        VALUE_STEPS = ((2, 2), (2, 3), (3, 2), (3, 3))
        QUANTISING = ((0, 1), (0, 2), (1, 1), (1, 3), (2, 1), (3, 1), (LAST, STEPS - 1))
        FLIPS = ((0, 1), (2, 3), (), ())
        FLIPS_FIRST = ((), (0,), (1, 2, 3), ())

        def tiles_to_turn(c, s):
            tiles = []
            if c < LAST:
                tiles += [(w_raws[c + 1], t) for t in (FLIPS_FIRST[s] if c == 0 else FLIPS[s])]
            if c == 1 and s >= 2:
                tiles += [(v_raw, 2 * s - 4), (v_raw, 2 * s - 3)]
            return tiles

        def new_products():
            return work.tile([P, 2, 2, CHUNK_HEADS, HEAD], F32, name="products")

        zeros = keep.tile([P, CHUNK], BF16)
        nc.vector.memset(zeros[:], 0.0)
        idle_sums = new_sums()

        def warm(times):
            for i in range(times):
                nc.tensor.matmul(idle_sums[:], lhsT=zeros[:, :P], rhs=zeros[:], start=True, stop=True)

        w_now = new_w(quant, 2)
        warm(5)
        flip_x(0)
        warm(1)
        flip_w(planes_of(w_raws[0], 0), 0, w_now, nc.vector.tensor_copy)
        flip_w(planes_of(w_raws[0], 1), 1, w_now, nc.scalar.copy)
        warm(1)
        quantize_x(0, 1)
        flip_x(1)
        warm(1)
        quantize_w(w_now, 0)
        quantize_x(1, 2)
        flip_w(planes_of(w_raws[0], 2), 2, w_now, nc.vector.tensor_copy)
        products = new_products()
        for part in range(2):
            h0, h1 = part * CHUNK_HEADS // 2, (part + 1) * CHUNK_HEADS // 2
            accs = [new_sums()[:, : CHUNK // 2] for i in range(2)]
            for i in range(2):
                project(accs[i], i, w_now, part)
            if part == 0:
                flip_w(planes_of(w_raws[0], 3), 3, w_now, nc.scalar.copy)
                for m in range(2, 5):
                    flip_x(m)
            multiply(accs[0], 0, products, 0, h0, h1)
            multiply(accs[1], 1, products, 1, h0, h1)
            if part == 0:
                quantize_w(w_now, 1)
                quantize_x(2, 4)

        w_value = new_w(keep, 1)
        planes_ahead = {}
        behind = None
        for c in range(len(rotated)):
            rows = rotated[c][1]
            w_next = new_w(quant, 1) if c < LAST else None
            for s in range(STEPS):
                m0 = 2 * s
                result = work.tile([P, 2, CHUNK_HEADS, HEAD], F32)
                if (c, s) != (0, 0):
                    products = new_products()
                turns = []
                if c == 0 and s + 2 < STEPS:
                    turns += [(flip_x, (m,)) for m in range(5 if s == 0 else m0 + 4, m0 + 6)]
                for n, (raw, t) in enumerate(tiles_to_turn(c, s)):
                    planes = planes_of(raw, t) if c == 0 else planes_ahead[(c, s)][n]
                    turns.append((flip_w, (planes, t, w_value if raw is v_raw else w_next, nc.scalar.copy)))
                later = divmod(c * STEPS + s + 2, STEPS)
                if later[0] > 0:
                    planes_ahead[later] = [ordered(raw, t) for raw, t in tiles_to_turn(later[0], later[1])]
                for i in range(2):
                    if (c, s) != (0, 0):
                        multiply(project_all(m0 + i, w_now)[:], m0 + i, products, i)
                    for turn, operands in turns[: len(turns) // 2] if i == 0 else turns[len(turns) // 2 :]:
                        turn(*operands)
                if c == 0 and s + 2 < STEPS:
                    quantize_x(m0 + 4, m0 + 6)
                if behind is not None:
                    add(nc.vector, behind[0], behind[1], GPSIMD_UNITS, UNITS)
                    store(behind[1], behind[2], behind[3], 0, 2)
                    behind = None
                if c < LAST and s == (2 if c == 0 else 1):
                    quantize_w(w_next, 0)
                if c == 1 and s == 3:
                    quantize_w(w_value, 0)
                if c == LAST and s == STEPS - 1:
                    for i in range(2):
                        add(nc.vector, products, result, i * CHUNK_HEADS, (i + 1) * CHUNK_HEADS)
                        store(result, rows, m0, i, i + 1)
                elif (c, s + 1) in QUANTISING:
                    add(nc.gpsimd, products, result, 0, UNITS)
                    store(result, rows, m0, 0, 2)
                else:
                    add(nc.gpsimd, products, result, 0, GPSIMD_UNITS)
                    behind = (products, result, rows, m0)
                if (c, s) in VALUE_STEPS:
                    for i in range(2):
                        project_value(2 * VALUE_STEPS.index((c, s)) + i, w_value)
            w_now = w_next
